import numpy as np
import ml_dtypes


def mxq(x, axis, fmt="e4m3"):
    dtype, down = {"e4m3": (ml_dtypes.float8_e4m3fn, 7), "e5m2": (ml_dtypes.float8_e5m2, 14)}[fmt]
    v = np.moveaxis(np.asarray(x, np.float32).astype(ml_dtypes.bfloat16).astype(np.float64), axis, -1)
    blocks = v.reshape(v.shape[:-1] + (-1, 32))
    amax = np.abs(blocks).max(-1, keepdims=True)
    byte = np.maximum(np.where(amax > 0, np.frexp(amax)[1] - 1 + 127, 0) - down, 1)
    scale = np.exp2(byte - 127.0)
    codes = (blocks / scale).astype(np.float32).astype(dtype).astype(np.float64)
    return np.moveaxis((codes * scale).reshape(v.shape), -1, axis)


WIDE = False


def mx_kscale(k):
    if not WIDE:
        return np.ones(k)
    levels = np.array([10, -10, 5, -5, 0])
    a = np.random.permutation(np.resize(levels, k // 512 * 4)).reshape(k // 512, 4)
    idx = np.arange(k)
    return np.exp2(a[idx // 512, idx % 128 // 32])


BF16 = ml_dtypes.bfloat16


def bf(x):
    return np.asarray(x, np.float32).astype(BF16)


def f64(x):
    return np.asarray(x).astype(np.float64)


E2M1 = np.array([0.0, 0.5, 1.0, 1.5, 2.0, 3.0, 4.0, 6.0, -0.0, -0.5, -1.0, -1.5, -2.0, -3.0, -4.0, -6.0])


def pack_weight(w, fmt):
    k, n = w.shape
    w = f64(bf(w)).reshape(k // 32, 32, n)
    amax = np.abs(w).max(1)
    if fmt == "e4m3":
        byte = np.frexp(amax)[1] - 1 + 127 - 7
    else:
        mant, ex = np.frexp(amax / 6.0)
        byte = np.where(mant > 0.5, ex, ex - 1) + 127
    byte = np.clip(np.where(amax > 0, byte, 1), 1, 254)
    scaled = (w * np.exp2(127.0 - byte)[:, None, :]).reshape(k, n).astype(np.float32)
    by_word = np.ascontiguousarray(scaled.reshape(k // 512, 128, 4, n).transpose(0, 1, 3, 2))
    if fmt == "e4m3":
        words = by_word.astype(ml_dtypes.float8_e4m3fn).view(np.uint8)
    else:
        c = by_word.astype(ml_dtypes.float4_e2m1fn).view(np.uint8) & 0xF
        words = c[..., 0::2] | (c[..., 1::2] << 4)
    return np.ascontiguousarray(words), np.ascontiguousarray(byte.astype(np.uint8).reshape(k // 512, 16, n))


def unpack_weight(words, scales, fmt):
    g, p, n, _ = words.shape
    if fmt == "e4m3":
        vals = np.ascontiguousarray(words).view(ml_dtypes.float8_e4m3fn).astype(np.float64)
    else:
        nib = np.empty((g, p, n, 4), np.uint8)
        nib[..., 0::2] = words & 0xF
        nib[..., 1::2] = words >> 4
        vals = E2M1[nib]
    vals = vals * np.repeat(np.exp2(scales.astype(np.float64) - 127.0), 8, axis=1)[..., None]
    return vals.transpose(0, 1, 3, 2).reshape(g * 512, n)


B, C_IN, H, W, HID, K, C_OUT = 2, 2048, 8, 8, 2048, 4, 2048


def setup_inputs():
    s = mx_kscale(C_IN)
    x = bf(np.random.standard_normal((B, C_IN, H, W)) * s[None, :, None, None])
    w_in = np.random.standard_normal((HID, C_IN)) / np.sqrt(C_IN) / s[None, :]
    w_in_words, w_in_scales = pack_weight(np.ascontiguousarray(w_in.T), "e4m3")
    return {
        "x": x,
        "w_in_words": w_in_words,
        "w_in_scales": w_in_scales,
        "b_in": bf(np.random.standard_normal(HID) * 0.3),
        "centers": bf(np.linspace(-2.0, 2.0, K).reshape(1, 1, K, 1, 1) + 0.1 * np.random.standard_normal((1, HID, K, 1, 1))),
        "log_widths": bf(np.random.standard_normal((1, HID, K, 1, 1)) * 0.3),
        "out_weight": bf(np.random.standard_normal((C_OUT, HID, K)) * 2.0 / np.sqrt(HID * K)),
        "out_bias": bf(np.random.standard_normal(C_OUT) * 0.3),
    }


def reference(x, w_in_words, w_in_scales, b_in, centers, log_widths, out_weight, out_bias):
    xq = mxq(f64(x), 1, "e4m3")
    z = (unpack_weight(w_in_words, w_in_scales, "e4m3").T @ xq.reshape(B, C_IN, H * W)).reshape(B, HID, H, W) + f64(b_in)[None, :, None, None]
    z = z[:, :, None, :, :]
    widths = np.logaddexp(f64(log_widths), 0.0) + 1e-4
    phi = np.exp(-(((z - f64(centers)) / widths) ** 2))
    pq = mxq(phi.reshape(B, HID * K, H * W), 1, "e4m3")
    out = (mxq(f64(out_weight).reshape(C_OUT, HID * K), 1, "e4m3") @ pq).reshape(B, C_OUT, H, W)
    return out + f64(out_bias)[None, :, None, None]

@@ -1,0 +1,318 @@
+from contextlib import ExitStack
+
+import concourse.mybir as mybir
+from concourse.masks import make_identity
+
+F32 = mybir.dt.float32
+BF16 = mybir.dt.bfloat16
+I32 = mybir.dt.int32
+U32 = mybir.dt.uint32
+U8 = mybir.dt.uint8
+FP8X4 = mybir.dt.float8_e4m3fn_x4
+ACT = mybir.ActivationFunctionType
+ALU = mybir.AluOpType
+
+BATCH, C_IN, HW, HID, KNOTS, C_OUT = 2, 2048, 64, 2048, 4, 2048
+PIX = BATCH * HW
+
+P = 128
+PACK = 4
+K_PASS = P * PACK
+BANK = 512
+PER_BANK = BANK // P
+
+PASSES_1 = C_IN // K_PASS
+PASSES_2 = HID * KNOTS // K_PASS
+SLABS = 2 * PASSES_2
+SLAB_CH = HID // SLABS
+
+HID_CHUNK = BANK
+HID_CHUNKS = HID // HID_CHUNK
+CHUNK_SLABS = HID_CHUNK // SLAB_CH
+CHUNK_PASSES = CHUNK_SLABS // 2
+
+TILES = C_OUT // P
+HALVES = 2
+HALF_WORDS = HID * KNOTS // 2 // HALVES
+HALF_PASSES = PASSES_2 // HALVES
+HALF_BANKS = HALF_WORDS // BANK
+
+STREAM_BUFS = 8
+BASIS_AHEAD = 2
+
+FLOPS = 2 * PIX * C_IN * HID + 2 * PIX * HID * KNOTS * C_OUT
+
+
+def tile_rbfkanhead_w_kernel(
+    tc, x, w_in_words, w_in_scales, b_in, centers, log_widths, out_weight, out_bias, out
+):
+    nc = tc.nc
+    with ExitStack() as ctx:
+        keep = ctx.enter_context(tc.tile_pool(name="keep", bufs=1))
+        stream = ctx.enter_context(tc.tile_pool(name="stream", bufs=STREAM_BUFS))
+        twice = ctx.enter_context(tc.tile_pool(name="twice", bufs=HID_CHUNKS))
+        work = ctx.enter_context(tc.tile_pool(name="work", bufs=2))
+        regroup = ctx.enter_context(tc.tile_pool(name="regroup", bufs=3))
+        packed = ctx.enter_context(tc.tile_pool(name="packed", bufs=8))
+        results = ctx.enter_context(tc.tile_pool(name="results", bufs=3))
+        banks = ctx.enter_context(tc.psum_pool(name="banks", bufs=7))
+        sums = ctx.enter_context(tc.psum_pool(name="sums", bufs=1))
+        ctx.enter_context(tc.manual_schedule())
+
+        w_in_chunk = {}
+        weight_half = {}
+
+        def load_w_in_chunk(j):
+            cols = slice(j * HID_CHUNK, (j + 1) * HID_CHUNK)
+            w_in_chunk[j] = stream.tile(
+                [P, PASSES_1, HID_CHUNK], I32, name="w_in_chunk%d" % j, tag="stream", align_bytes=64
+            )
+            nc.sync.dma_start(
+                out=w_in_chunk[j][:],
+                in_=w_in_words[:, :, cols, :].rearrange("g p n t -> p g (n t)").bitcast(I32),
+            )
+
+        def load_weight_half(h):
+            rows = slice((h // HALVES) * P, (h // HALVES + 1) * P)
+            chans = slice((h % HALVES) * (HID // HALVES), (h % HALVES + 1) * (HID // HALVES))
+            weight_half[h] = stream.tile(
+                [P, HALF_WORDS], F32, name="weight_half%d" % h, tag="stream", align_bytes=64
+            )
+            nc.sync.dma_start(
+                out=weight_half[h][:].bitcast(BF16),
+                in_=out_weight[rows, chans, :].rearrange("o c k -> o (c k)"),
+            )
+
+        x_rows = keep.tile([P, BATCH, PASSES_1, PACK, HW], BF16)
+        for b in range(BATCH):
+            nc.sync.dma_start(
+                out=x_rows[:, b].rearrange("p g t x -> p g (t x)"),
+                in_=x[b].rearrange("(g p t) h w -> p g (t h w)", g=PASSES_1, p=P, t=PACK),
+            )
+
+        w_in_planes = keep.tile([P, HID], U8, align_bytes=64)
+        nc.vector.memset(w_in_planes[:].bitcast(I32), 0)
+        for quarter in range(4):
+            nc.sync.dma_start(
+                out=w_in_planes[32 * quarter : 32 * quarter + 16, :].bitcast(I32),
+                in_=w_in_scales[:, 4 * quarter : 4 * quarter + 4, :].bitcast(I32),
+            )
+
+        for j in range(HID_CHUNKS):
+            load_w_in_chunk(j)
+        for h in range(STREAM_BUFS - HID_CHUNKS):
+            load_weight_half(h)
+
+        square = keep.tile([P, P], F32)
+        nc.vector.memset(square[:], 0.0)
+        b_in_rows = keep.tile([P, SLAB_CH], BF16)
+        out_bias_rows = keep.tile([P, P], BF16)
+        nc.scalar.dma_start(
+            out=square[0:32, :].bitcast(BF16),
+            in_=centers.rearrange("a (s c) k h w -> (a s) (c k h w)", s=SLABS),
+        )
+        nc.scalar.dma_start(
+            out=square[32:64, :].bitcast(BF16),
+            in_=log_widths.rearrange("a (s c) k h w -> (a s) (c k h w)", s=SLABS),
+        )
+        nc.scalar.dma_start(out=b_in_rows[64:96, :], in_=b_in.rearrange("(s c) -> s c", s=SLABS))
+        nc.scalar.dma_start(out=out_bias_rows[96:112, :], in_=out_bias.rearrange("(i o) -> i o", i=TILES))
+        nc.vector.tensor_copy(
+            out=square[64:96, :].rearrange("s (c d) -> s c d", d=2),
+            in_=b_in_rows[64:96, :].unsqueeze(2).to_broadcast([32, SLAB_CH, 2]),
+        )
+        nc.vector.tensor_copy(out=square[96:112, :], in_=out_bias_rows[96:112, :])
+
+        ident = keep.tile([P, P], F32)
+        make_identity(nc, ident[:])
+        square_t = banks.tile([P, BANK], F32, name="square_t", tag="bank")
+        nc.tensor.transpose(square_t[:, 0:P], square[:], ident[:])
+        columns = keep.tile([P, P], F32)
+        nc.vector.tensor_copy(out=columns[:], in_=square_t[:, 0:P])
+        centers_col = columns[:, 0:32].bitcast(BF16)
+        log_widths_col = columns[:, 32:64].bitcast(BF16)
+        b_in_col = columns[:, 64:96]
+        out_bias_col = columns[:, 96:112]
+
+        x_grouped = keep.tile([P, PASSES_1, PIX, PACK], BF16, align_bytes=64)
+        for b in range(BATCH):
+            nc.vector.tensor_copy(
+                out=x_grouped[:, :, b * HW : (b + 1) * HW, :],
+                in_=x_rows[:, b].rearrange("p g t x -> p g x t"),
+            )
+        x_codes = keep.tile([P, PASSES_1 * PIX], U32, align_bytes=64)
+        x_planes = keep.tile([P, PASSES_1 * PIX], U8, align_bytes=64)
+        nc.vector.quantize_mx(
+            out=x_codes[:].bitcast(FP8X4),
+            scales=x_planes[:],
+            in_=x_grouped[:].rearrange("p g x t -> p (g x t)"),
+        )
+
+        soft = keep.tile([P, 2 * SLABS], F32)
+        nc.scalar.activation(out=soft[:], in_=log_widths_col, func=ACT.Abs)
+        nc.scalar.activation(out=soft[:], in_=soft[:], func=ACT.Exp, scale=-1.0)
+        nc.scalar.activation(out=soft[:], in_=soft[:], func=ACT.Ln, bias=1.0)
+        width = keep.tile([P, 2 * SLABS], F32)
+        nc.vector.tensor_scalar(out=width[:], in0=log_widths_col, scalar1=0.0, scalar2=None, op0=ALU.max)
+        nc.vector.tensor_tensor(out=width[:], in0=width[:], in1=soft[:], op=ALU.add)
+        nc.vector.tensor_scalar(out=width[:], in0=width[:], scalar1=1e-4, scalar2=None, op0=ALU.add)
+        inv_width = keep.tile([P, 2 * SLABS], F32)
+        nc.vector.reciprocal(out=inv_width[:], in_=width[:])
+        offset = keep.tile([P, 2 * SLABS], F32)
+        nc.vector.tensor_tensor(
+            out=offset[:].rearrange("p (s e) -> p s e", e=2),
+            in0=b_in_col.unsqueeze(2).to_broadcast([P, SLABS, 2]),
+            in1=centers_col.rearrange("p (s e) -> p s e", e=2),
+            op=ALU.subtract,
+        )
+        nc.vector.tensor_tensor(out=offset[:], in0=offset[:], in1=inv_width[:], op=ALU.mult)
+
+        z_twice = {}
+        phi = keep.tile([P, PASSES_2, PIX, PACK], BF16, align_bytes=64)
+        phi_codes = keep.tile([P, PASSES_2 * PIX], U32, align_bytes=64)
+        phi_planes = keep.tile([P, PASSES_2 * PIX], U8, align_bytes=64)
+
+        def first_product(j):
+            cols = slice(j * HID_CHUNK, (j + 1) * HID_CHUNK)
+            z_bank = banks.tile([P, BANK], F32, name="z_bank", tag="bank")
+            for g in range(PASSES_1):
+                nc.tensor.matmul_mx(
+                    out=z_bank[:],
+                    lhsT=x_codes[:, g * PIX : (g + 1) * PIX].bitcast(FP8X4),
+                    lhsT_scale=x_planes[:, g * PIX : (g + 1) * PIX],
+                    rhs=w_in_chunk[j][:, g, :].bitcast(FP8X4),
+                    rhs_scale=w_in_planes[4 * g : P, cols],
+                    start=(g == 0),
+                    stop=(g == PASSES_1 - 1),
+                )
+            z_twice[j] = twice.tile([P, 2 * HID_CHUNK], F32, name="z_twice")
+            nc.vector.tensor_copy(
+                out=z_twice[j][:].rearrange("x (c d) -> x c d", d=2),
+                in_=z_bank[:].unsqueeze(2).to_broadcast([P, HID_CHUNK, 2]),
+            )
+            load_weight_half(STREAM_BUFS - HID_CHUNKS + j)
+
+        def basis(j):
+            squares = work.tile([P, CHUNK_PASSES, PACK, PIX], F32, name="squares")
+            for first in range(0, CHUNK_SLABS, PER_BANK):
+                z_t = banks.tile([P, PER_BANK, PIX], F32, name="z_t", tag="bank")
+                for m in range(PER_BANK):
+                    nc.tensor.transpose(
+                        z_t[:, m, :], z_twice[j][:, (first + m) * P : (first + m + 1) * P], ident[:]
+                    )
+                for m in range(PER_BANK):
+                    g_local, u = divmod(first + m, 2)
+                    for e in range(2):
+                        col = 2 * (j * CHUNK_SLABS + first + m) + e
+                        nc.scalar.activation(
+                            out=squares[:, g_local, 2 * u + e, :],
+                            in_=z_t[:, m, :],
+                            func=ACT.Square,
+                            scale=inv_width[:, col : col + 1],
+                            bias=offset[:, col : col + 1],
+                        )
+            for g_local in range(CHUNK_PASSES):
+                nc.scalar.activation(
+                    out=phi[:, j * CHUNK_PASSES + g_local, :, :],
+                    in_=squares[:, g_local].rearrange("p t x -> p x t"),
+                    func=ACT.Exp,
+                    scale=-1.0,
+                )
+
+        def quantise_phi(j):
+            passes = slice(j * CHUNK_PASSES, (j + 1) * CHUNK_PASSES)
+            cols = slice(j * CHUNK_PASSES * PIX, (j + 1) * CHUNK_PASSES * PIX)
+            nc.vector.quantize_mx(
+                out=phi_codes[:, cols].bitcast(FP8X4),
+                scales=phi_planes[:, cols],
+                in_=phi[:, passes].rearrange("p g x t -> p (g x t)"),
+            )
+
+        grouped = {}
+        weight_codes = {}
+        weight_planes = {}
+        sum_bank = sums.tile([P, PER_BANK, PIX], F32)
+
+        def quantise_weight(h):
+            weight_codes[h] = packed.tile([P, HALF_PASSES * P], U32, name="weight_codes", align_bytes=64)
+            weight_planes[h] = packed.tile([P, HALF_PASSES * P], U8, name="weight_planes", align_bytes=64)
+            nc.vector.quantize_mx(
+                out=weight_codes[h][:].bitcast(FP8X4),
+                scales=weight_planes[h][:],
+                in_=grouped[h][:].bitcast(BF16),
+            )
+
+        def prepare(h, scalar_helps):
+            grouped[h] = regroup.tile([P, HALF_WORDS], F32, name="grouped", align_bytes=64)
+            for b in range(HALF_BANKS):
+                w_t = banks.tile([P, 2, 2, P], F32, name="w_t", tag="bank")
+                for m in range(PER_BANK):
+                    n = b * PER_BANK + m
+                    nc.tensor.transpose(
+                        w_t[:, m // 2, m % 2, :], weight_half[h][:, n * P : (n + 1) * P], ident[:]
+                    )
+                dst = grouped[h][:, b * BANK : (b + 1) * BANK].rearrange("p (g o u) -> p g o u", g=2, u=2)
+                src = w_t[:].rearrange("p g u o -> p g o u")
+                if scalar_helps and b > 0:
+                    nc.scalar.copy(out=dst, in_=src)
+                else:
+                    nc.vector.tensor_copy(out=dst, in_=src)
+                if b == 0 and h > 0:
+                    quantise_weight(h - 1)
+            if h + STREAM_BUFS < TILES * HALVES:
+                load_weight_half(h + STREAM_BUFS)
+
+        def multiply(i):
+            for g in range(PASSES_2):
+                h = i * HALVES + g // HALF_PASSES
+                cols = slice((g % HALF_PASSES) * P, (g % HALF_PASSES + 1) * P)
+                nc.tensor.matmul_mx(
+                    out=sum_bank[:, i % PER_BANK, :],
+                    lhsT=weight_codes[h][:, cols].bitcast(FP8X4),
+                    lhsT_scale=weight_planes[h][:, cols],
+                    rhs=phi_codes[:, g * PIX : (g + 1) * PIX].bitcast(FP8X4),
+                    rhs_scale=phi_planes[:, g * PIX : (g + 1) * PIX],
+                    start=(g == 0),
+                    stop=(g == PASSES_2 - 1),
+                )
+
+        def finish(i):
+            result = results.tile([P, PIX], F32, name="result")
+            nc.scalar.activation(
+                out=result[:], in_=sum_bank[:, i % PER_BANK, :], func=ACT.Identity, bias=out_bias_col[:, i : i + 1]
+            )
+            nc.scalar.dma_start(
+                out=out[:, i * P : (i + 1) * P].rearrange("b o h w -> o b (h w)"),
+                in_=result[:].rearrange("o (b x) -> o b x", b=BATCH),
+            )
+
+        for j in range(HID_CHUNKS):
+            first_product(j)
+            if j < BASIS_AHEAD:
+                basis(j)
+
+        phi_done = 0
+        multiplied = 0
+        finished = 0
+        for i in range(TILES):
+            for t in range(finished, multiplied):
+                finish(t)
+            finished = multiplied
+            scalar_helps = i + BASIS_AHEAD >= HID_CHUNKS
+            for half in range(HALVES):
+                prepare(i * HALVES + half, scalar_helps)
+            for j in range(phi_done, min(i + BASIS_AHEAD, HID_CHUNKS)):
+                quantise_phi(j)
+            phi_done = min(i + BASIS_AHEAD, HID_CHUNKS)
+            if i + BASIS_AHEAD < HID_CHUNKS:
+                basis(i + BASIS_AHEAD)
+            if phi_done == HID_CHUNKS:
+                for t in range(multiplied, i):
+                    multiply(t)
+                multiplied = i
+
+        for t in range(finished, multiplied):
+            finish(t)
+        quantise_weight(TILES * HALVES - 1)
+        multiply(TILES - 1)
+        finish(TILES - 1)

@@ -37,8 +37,9 @@ HALF_WORDS = HID * KNOTS // 2 // HALVES
 HALF_PASSES = PASSES_2 // HALVES
 HALF_BANKS = HALF_WORDS // BANK
 
-STREAM_BUFS = 8
+STREAM_BUFS = 6
 BASIS_AHEAD = 2
+EARLY_TILES = 3
 
 FLOPS = 2 * PIX * C_IN * HID + 2 * PIX * HID * KNOTS * C_OUT
 
@@ -52,7 +53,7 @@ def tile_rbfkanhead_w_kernel(
         stream = ctx.enter_context(tc.tile_pool(name="stream", bufs=STREAM_BUFS))
         twice = ctx.enter_context(tc.tile_pool(name="twice", bufs=HID_CHUNKS))
         work = ctx.enter_context(tc.tile_pool(name="work", bufs=2))
-        regroup = ctx.enter_context(tc.tile_pool(name="regroup", bufs=3))
+        regroup = ctx.enter_context(tc.tile_pool(name="regroup", bufs=EARLY_TILES * HALVES + 1))
         packed = ctx.enter_context(tc.tile_pool(name="packed", bufs=8))
         results = ctx.enter_context(tc.tile_pool(name="results", bufs=3))
         banks = ctx.enter_context(tc.psum_pool(name="banks", bufs=7))
@@ -152,6 +153,8 @@ def tile_rbfkanhead_w_kernel(
         nc.scalar.activation(out=soft[:], in_=log_widths_col, func=ACT.Abs)
         nc.scalar.activation(out=soft[:], in_=soft[:], func=ACT.Exp, scale=-1.0)
         nc.scalar.activation(out=soft[:], in_=soft[:], func=ACT.Ln, bias=1.0)
+        exp_again = keep.tile([P, 1], F32)
+        nc.scalar.activation(out=exp_again[:], in_=soft[:, 0:1], func=ACT.Exp)
         width = keep.tile([P, 2 * SLABS], F32)
         nc.vector.tensor_scalar(out=width[:], in0=log_widths_col, scalar1=0.0, scalar2=None, op0=ALU.max)
         nc.vector.tensor_tensor(out=width[:], in0=width[:], in1=soft[:], op=ALU.add)
@@ -233,16 +236,19 @@ def tile_rbfkanhead_w_kernel(
         weight_planes = {}
         sum_bank = sums.tile([P, PER_BANK, PIX], F32)
 
-        def quantise_weight(h):
+        def quantise_weight(h, pieces):
             weight_codes[h] = packed.tile([P, HALF_PASSES * P], U32, name="weight_codes", align_bytes=64)
             weight_planes[h] = packed.tile([P, HALF_PASSES * P], U8, name="weight_planes", align_bytes=64)
-            nc.vector.quantize_mx(
-                out=weight_codes[h][:].bitcast(FP8X4),
-                scales=weight_planes[h][:],
-                in_=grouped[h][:].bitcast(BF16),
-            )
+            for n in range(pieces):
+                words = slice(n * HALF_PASSES * P // pieces, (n + 1) * HALF_PASSES * P // pieces)
+                pairs = slice(n * HALF_WORDS // pieces, (n + 1) * HALF_WORDS // pieces)
+                nc.vector.quantize_mx(
+                    out=weight_codes[h][:, words].bitcast(FP8X4),
+                    scales=weight_planes[h][:, words],
+                    in_=grouped[h][:, pairs].bitcast(BF16),
+                )
 
-        def prepare(h, scalar_helps):
+        def prepare(h, vector_banks, due):
             grouped[h] = regroup.tile([P, HALF_WORDS], F32, name="grouped", align_bytes=64)
             for b in range(HALF_BANKS):
                 w_t = banks.tile([P, 2, 2, P], F32, name="w_t", tag="bank")
@@ -253,12 +259,13 @@ def tile_rbfkanhead_w_kernel(
                     )
                 dst = grouped[h][:, b * BANK : (b + 1) * BANK].rearrange("p (g o u) -> p g o u", g=2, u=2)
                 src = w_t[:].rearrange("p g u o -> p g o u")
-                if scalar_helps and b > 0:
-                    nc.scalar.copy(out=dst, in_=src)
-                else:
+                if b < vector_banks:
                     nc.vector.tensor_copy(out=dst, in_=src)
-                if b == 0 and h > 0:
-                    quantise_weight(h - 1)
+                else:
+                    nc.scalar.copy(out=dst, in_=src)
+                if b == 0:
+                    for earlier in due:
+                        quantise_weight(earlier, 1)
             if h + STREAM_BUFS < TILES * HALVES:
                 load_weight_half(h + STREAM_BUFS)
 
@@ -292,27 +299,38 @@ def tile_rbfkanhead_w_kernel(
                 basis(j)
 
         phi_done = 0
+        quantised = 0
         multiplied = 0
         finished = 0
         for i in range(TILES):
             for t in range(finished, multiplied):
                 finish(t)
             finished = multiplied
-            scalar_helps = i + BASIS_AHEAD >= HID_CHUNKS
-            for half in range(HALVES):
-                prepare(i * HALVES + half, scalar_helps)
+            for h in range(i * HALVES, (i + 1) * HALVES):
+                if i < EARLY_TILES:
+                    prepare(h, HALF_BANKS, [])
+                elif h - quantised > 1:
+                    prepare(h, 0, [quantised, quantised + 1])
+                    quantised += 2
+                else:
+                    prepare(h, 1, [quantised])
+                    quantised += 1
+            if i == EARLY_TILES - 1:
+                for h in range(HALVES):
+                    quantise_weight(h, 1)
+                quantised = HALVES
             for j in range(phi_done, min(i + BASIS_AHEAD, HID_CHUNKS)):
                 quantise_phi(j)
             phi_done = min(i + BASIS_AHEAD, HID_CHUNKS)
             if i + BASIS_AHEAD < HID_CHUNKS:
                 basis(i + BASIS_AHEAD)
             if phi_done == HID_CHUNKS:
-                for t in range(multiplied, i):
+                for t in range(multiplied, min(i, quantised // HALVES)):
                     multiply(t)
-                multiplied = i
+                multiplied = max(multiplied, min(i, quantised // HALVES))
 
         for t in range(finished, multiplied):
             finish(t)
-        quantise_weight(TILES * HALVES - 1)
+        quantise_weight(TILES * HALVES - 1, HALF_BANKS)
         multiply(TILES - 1)
         finish(TILES - 1)

@@ -28,18 +28,21 @@ SLAB_CH = HID // SLABS
 
 HID_CHUNK = BANK
 HID_CHUNKS = HID // HID_CHUNK
-CHUNK_SLABS = HID_CHUNK // SLAB_CH
-CHUNK_PASSES = CHUNK_SLABS // 2
+CHUNK_PASSES = PASSES_2 // HID_CHUNKS
+UNITS = SLABS // PER_BANK
+UNIT_PASSES = PASSES_2 // UNITS
+CHUNK_UNITS = UNITS // HID_CHUNKS
 
 TILES = C_OUT // P
-HALVES = 2
-HALF_WORDS = HID * KNOTS // 2 // HALVES
-HALF_PASSES = PASSES_2 // HALVES
-HALF_BANKS = HALF_WORDS // BANK
+SWEEPS = 2
+BLOCKS = SWEEPS * TILES
+BLOCK_WORDS = HID * KNOTS // 2 // SWEEPS
+BLOCK_PASSES = PASSES_2 // SWEEPS
+BLOCK_BANKS = BLOCK_WORDS // BANK
 
-STREAM_BUFS = 6
-BASIS_AHEAD = 2
-EARLY_TILES = 3
+RUN = 2
+STREAM_BUFS = 8
+PHI_EVERY = TILES // (UNITS // SWEEPS)
 
 FLOPS = 2 * PIX * C_IN * HID + 2 * PIX * HID * KNOTS * C_OUT
 
@@ -53,15 +56,14 @@ def tile_rbfkanhead_w_kernel(
         stream = ctx.enter_context(tc.tile_pool(name="stream", bufs=STREAM_BUFS))
         twice = ctx.enter_context(tc.tile_pool(name="twice", bufs=HID_CHUNKS))
         work = ctx.enter_context(tc.tile_pool(name="work", bufs=2))
-        regroup = ctx.enter_context(tc.tile_pool(name="regroup", bufs=EARLY_TILES * HALVES + 1))
-        packed = ctx.enter_context(tc.tile_pool(name="packed", bufs=8))
-        results = ctx.enter_context(tc.tile_pool(name="results", bufs=3))
+        regroup = ctx.enter_context(tc.tile_pool(name="regroup", bufs=2 * RUN))
+        packed = ctx.enter_context(tc.tile_pool(name="packed", bufs=3 * RUN))
         banks = ctx.enter_context(tc.psum_pool(name="banks", bufs=7))
         sums = ctx.enter_context(tc.psum_pool(name="sums", bufs=1))
         ctx.enter_context(tc.manual_schedule())
 
         w_in_chunk = {}
-        weight_half = {}
+        weight_block = {}
 
         def load_w_in_chunk(j):
             cols = slice(j * HID_CHUNK, (j + 1) * HID_CHUNK)
@@ -73,14 +75,15 @@ def tile_rbfkanhead_w_kernel(
                 in_=w_in_words[:, :, cols, :].rearrange("g p n t -> p g (n t)").bitcast(I32),
             )
 
-        def load_weight_half(h):
-            rows = slice((h // HALVES) * P, (h // HALVES + 1) * P)
-            chans = slice((h % HALVES) * (HID // HALVES), (h % HALVES + 1) * (HID // HALVES))
-            weight_half[h] = stream.tile(
-                [P, HALF_WORDS], F32, name="weight_half%d" % h, tag="stream", align_bytes=64
+        def load_weight_block(k):
+            sweep, tile_i = divmod(k, TILES)
+            rows = slice(tile_i * P, (tile_i + 1) * P)
+            chans = slice(sweep * (HID // SWEEPS), (sweep + 1) * (HID // SWEEPS))
+            weight_block[k] = stream.tile(
+                [P, BLOCK_WORDS], F32, name="weight_block%d" % k, tag="stream", align_bytes=64
             )
             nc.sync.dma_start(
-                out=weight_half[h][:].bitcast(BF16),
+                out=weight_block[k][:].bitcast(BF16),
                 in_=out_weight[rows, chans, :].rearrange("o c k -> o (c k)"),
             )
 
@@ -101,8 +104,8 @@ def tile_rbfkanhead_w_kernel(
 
         for j in range(HID_CHUNKS):
             load_w_in_chunk(j)
-        for h in range(STREAM_BUFS - HID_CHUNKS):
-            load_weight_half(h)
+        for k in range(STREAM_BUFS - HID_CHUNKS):
+            load_weight_block(k)
 
         square = keep.tile([P, P], F32)
         nc.vector.memset(square[:], 0.0)
@@ -193,30 +196,29 @@ def tile_rbfkanhead_w_kernel(
                 out=z_twice[j][:].rearrange("x (c d) -> x c d", d=2),
                 in_=z_bank[:].unsqueeze(2).to_broadcast([P, HID_CHUNK, 2]),
             )
-            load_weight_half(STREAM_BUFS - HID_CHUNKS + j)
+            load_weight_block(STREAM_BUFS - HID_CHUNKS + j)
 
-        def basis(j):
-            squares = work.tile([P, CHUNK_PASSES, PACK, PIX], F32, name="squares")
-            for first in range(0, CHUNK_SLABS, PER_BANK):
-                z_t = banks.tile([P, PER_BANK, PIX], F32, name="z_t", tag="bank")
-                for m in range(PER_BANK):
-                    nc.tensor.transpose(
-                        z_t[:, m, :], z_twice[j][:, (first + m) * P : (first + m + 1) * P], ident[:]
+        def basis(n):
+            j, part = divmod(n, CHUNK_UNITS)
+            z_t = banks.tile([P, PER_BANK, PIX], F32, name="z_t", tag="bank")
+            for m in range(PER_BANK):
+                col = (part * PER_BANK + m) * P
+                nc.tensor.transpose(z_t[:, m, :], z_twice[j][:, col : col + P], ident[:])
+            squares = work.tile([P, UNIT_PASSES, PACK, PIX], F32, name="squares")
+            for m in range(PER_BANK):
+                g_local, u = divmod(m, 2)
+                for e in range(2):
+                    col = 2 * (n * PER_BANK + m) + e
+                    nc.scalar.activation(
+                        out=squares[:, g_local, 2 * u + e, :],
+                        in_=z_t[:, m, :],
+                        func=ACT.Square,
+                        scale=inv_width[:, col : col + 1],
+                        bias=offset[:, col : col + 1],
                     )
-                for m in range(PER_BANK):
-                    g_local, u = divmod(first + m, 2)
-                    for e in range(2):
-                        col = 2 * (j * CHUNK_SLABS + first + m) + e
-                        nc.scalar.activation(
-                            out=squares[:, g_local, 2 * u + e, :],
-                            in_=z_t[:, m, :],
-                            func=ACT.Square,
-                            scale=inv_width[:, col : col + 1],
-                            bias=offset[:, col : col + 1],
-                        )
-            for g_local in range(CHUNK_PASSES):
+            for g_local in range(UNIT_PASSES):
                 nc.scalar.activation(
-                    out=phi[:, j * CHUNK_PASSES + g_local, :, :],
+                    out=phi[:, n * UNIT_PASSES + g_local, :, :],
                     in_=squares[:, g_local].rearrange("p t x -> p x t"),
                     func=ACT.Exp,
                     scale=-1.0,
@@ -235,102 +237,115 @@ def tile_rbfkanhead_w_kernel(
         weight_codes = {}
         weight_planes = {}
         sum_bank = sums.tile([P, PER_BANK, PIX], F32)
+        result = keep.tile([P, TILES, PIX], F32)
 
-        def quantise_weight(h, pieces):
-            weight_codes[h] = packed.tile([P, HALF_PASSES * P], U32, name="weight_codes", align_bytes=64)
-            weight_planes[h] = packed.tile([P, HALF_PASSES * P], U8, name="weight_planes", align_bytes=64)
+        def quantise_weight(k, pieces):
+            weight_codes[k] = packed.tile([P, BLOCK_PASSES * P], U32, name="weight_codes", align_bytes=64)
+            weight_planes[k] = packed.tile([P, BLOCK_PASSES * P], U8, name="weight_planes", align_bytes=64)
             for n in range(pieces):
-                words = slice(n * HALF_PASSES * P // pieces, (n + 1) * HALF_PASSES * P // pieces)
-                pairs = slice(n * HALF_WORDS // pieces, (n + 1) * HALF_WORDS // pieces)
+                words = slice(n * BLOCK_PASSES * P // pieces, (n + 1) * BLOCK_PASSES * P // pieces)
+                pairs = slice(n * BLOCK_WORDS // pieces, (n + 1) * BLOCK_WORDS // pieces)
                 nc.vector.quantize_mx(
-                    out=weight_codes[h][:, words].bitcast(FP8X4),
-                    scales=weight_planes[h][:, words],
-                    in_=grouped[h][:, pairs].bitcast(BF16),
+                    out=weight_codes[k][:, words].bitcast(FP8X4),
+                    scales=weight_planes[k][:, words],
+                    in_=grouped[k][:, pairs].bitcast(BF16),
                 )
 
-        def prepare(h, vector_banks, due):
-            grouped[h] = regroup.tile([P, HALF_WORDS], F32, name="grouped", align_bytes=64)
-            for b in range(HALF_BANKS):
+        def prepare(k, vector_banks):
+            grouped[k] = regroup.tile([P, BLOCK_WORDS], F32, name="grouped", align_bytes=64)
+            for b in range(BLOCK_BANKS):
                 w_t = banks.tile([P, 2, 2, P], F32, name="w_t", tag="bank")
                 for m in range(PER_BANK):
                     n = b * PER_BANK + m
                     nc.tensor.transpose(
-                        w_t[:, m // 2, m % 2, :], weight_half[h][:, n * P : (n + 1) * P], ident[:]
+                        w_t[:, m // 2, m % 2, :], weight_block[k][:, n * P : (n + 1) * P], ident[:]
                     )
-                dst = grouped[h][:, b * BANK : (b + 1) * BANK].rearrange("p (g o u) -> p g o u", g=2, u=2)
+                dst = grouped[k][:, b * BANK : (b + 1) * BANK].rearrange("p (g o u) -> p g o u", g=2, u=2)
                 src = w_t[:].rearrange("p g u o -> p g o u")
                 if b < vector_banks:
                     nc.vector.tensor_copy(out=dst, in_=src)
                 else:
                     nc.scalar.copy(out=dst, in_=src)
-                if b == 0:
-                    for earlier in due:
-                        quantise_weight(earlier, 1)
-            if h + STREAM_BUFS < TILES * HALVES:
-                load_weight_half(h + STREAM_BUFS)
+                if b == 0 and k > 0:
+                    quantise_weight(k - 1, 1)
+            if k + STREAM_BUFS < BLOCKS:
+                load_weight_block(k + STREAM_BUFS)
 
-        def multiply(i):
-            for g in range(PASSES_2):
-                h = i * HALVES + g // HALF_PASSES
-                cols = slice((g % HALF_PASSES) * P, (g % HALF_PASSES + 1) * P)
+        def multiply(k):
+            first_pass = (k // TILES) * BLOCK_PASSES
+            for g in range(BLOCK_PASSES):
+                cols = slice(g * P, (g + 1) * P)
+                pixels = slice((first_pass + g) * PIX, (first_pass + g + 1) * PIX)
                 nc.tensor.matmul_mx(
-                    out=sum_bank[:, i % PER_BANK, :],
-                    lhsT=weight_codes[h][:, cols].bitcast(FP8X4),
-                    lhsT_scale=weight_planes[h][:, cols],
-                    rhs=phi_codes[:, g * PIX : (g + 1) * PIX].bitcast(FP8X4),
-                    rhs_scale=phi_planes[:, g * PIX : (g + 1) * PIX],
+                    out=sum_bank[:, k % PER_BANK, :],
+                    lhsT=weight_codes[k][:, cols].bitcast(FP8X4),
+                    lhsT_scale=weight_planes[k][:, cols],
+                    rhs=phi_codes[:, pixels].bitcast(FP8X4),
+                    rhs_scale=phi_planes[:, pixels],
                     start=(g == 0),
-                    stop=(g == PASSES_2 - 1),
+                    stop=(g == BLOCK_PASSES - 1),
                 )
 
-        def finish(i):
-            result = results.tile([P, PIX], F32, name="result")
-            nc.scalar.activation(
-                out=result[:], in_=sum_bank[:, i % PER_BANK, :], func=ACT.Identity, bias=out_bias_col[:, i : i + 1]
-            )
-            nc.scalar.dma_start(
-                out=out[:, i * P : (i + 1) * P].rearrange("b o h w -> o b (h w)"),
-                in_=result[:].rearrange("o (b x) -> o b x", b=BATCH),
+        def collect(k):
+            sweep, tile_i = divmod(k, TILES)
+            if sweep == 0:
+                nc.scalar.activation(
+                    out=result[:, tile_i, :],
+                    in_=sum_bank[:, k % PER_BANK, :],
+                    func=ACT.Identity,
+                    bias=out_bias_col[:, tile_i : tile_i + 1],
+                )
+            else:
+                nc.vector.tensor_tensor(
+                    out=result[:, tile_i, :],
+                    in0=sum_bank[:, k % PER_BANK, :],
+                    in1=result[:, tile_i, :],
+                    op=ALU.add,
+                )
+
+        def store(tile_i):
+            nc.sync.dma_start(
+                out=out[:, tile_i * P : (tile_i + 1) * P].rearrange("b o h w -> o b (h w)"),
+                in_=result[:, tile_i, :].rearrange("o (b x) -> o b x", b=BATCH),
             )
 
         for j in range(HID_CHUNKS):
             first_product(j)
-            if j < BASIS_AHEAD:
-                basis(j)
+            if j < HID_CHUNKS // SWEEPS:
+                for n in range(j * CHUNK_UNITS, (j + 1) * CHUNK_UNITS):
+                    basis(n)
 
-        phi_done = 0
-        quantised = 0
-        multiplied = 0
-        finished = 0
-        for i in range(TILES):
-            for t in range(finished, multiplied):
-                finish(t)
-            finished = multiplied
-            for h in range(i * HALVES, (i + 1) * HALVES):
-                if i < EARLY_TILES:
-                    prepare(h, HALF_BANKS, [])
-                elif h - quantised > 1:
-                    prepare(h, 0, [quantised, quantised + 1])
-                    quantised += 2
-                else:
-                    prepare(h, 1, [quantised])
-                    quantised += 1
-            if i == EARLY_TILES - 1:
-                for h in range(HALVES):
-                    quantise_weight(h, 1)
-                quantised = HALVES
-            for j in range(phi_done, min(i + BASIS_AHEAD, HID_CHUNKS)):
+        units_done = UNITS // SWEEPS
+        chunks_done = 0
+        stored = 0
+        for first in range(0, BLOCKS, RUN):
+            for k in range(max(first - 2 * RUN, 0), max(first - RUN, 0)):
+                collect(k)
+            chunks_ready = units_done // CHUNK_UNITS
+            for k in range(first, first + RUN):
+                with_phi = k < TILES and k % PHI_EVERY == PHI_EVERY - 1
+                prepare(k, BLOCK_BANKS if k == 0 or with_phi else 1)
+                if with_phi:
+                    basis(units_done)
+                    units_done += 1
+            for j in range(chunks_done, chunks_ready):
                 quantise_phi(j)
-            phi_done = min(i + BASIS_AHEAD, HID_CHUNKS)
-            if i + BASIS_AHEAD < HID_CHUNKS:
-                basis(i + BASIS_AHEAD)
-            if phi_done == HID_CHUNKS:
-                for t in range(multiplied, min(i, quantised // HALVES)):
-                    multiply(t)
-                multiplied = max(multiplied, min(i, quantised // HALVES))
+            chunks_done = chunks_ready
+            for k in range(max(first - RUN, 0), first):
+                multiply(k)
+            if first + RUN + STREAM_BUFS >= BLOCKS:
+                for tile_i in range(stored, max(first - 2 * RUN - TILES, 0)):
+                    store(tile_i)
+                stored = max(first - 2 * RUN - TILES, stored)
 
-        for t in range(finished, multiplied):
-            finish(t)
-        quantise_weight(TILES * HALVES - 1, HALF_BANKS)
-        multiply(TILES - 1)
-        finish(TILES - 1)
+        quantise_weight(BLOCKS - 1, BLOCK_BANKS)
+        for k in range(BLOCKS - 2 * RUN, BLOCKS - RUN):
+            collect(k)
+        for tile_i in range(stored, TILES - RUN):
+            store(tile_i)
+        for k in range(BLOCKS - RUN, BLOCKS):
+            multiply(k)
+        for k in range(BLOCKS - RUN, BLOCKS):
+            collect(k)
+        for tile_i in range(TILES - RUN, TILES):
+            store(tile_i)

@@ -324,7 +324,7 @@ def tile_rbfkanhead_w_kernel(
             chunks_ready = units_done // CHUNK_UNITS
             for k in range(first, first + RUN):
                 with_phi = k < TILES and k % PHI_EVERY == PHI_EVERY - 1
-                prepare(k, BLOCK_BANKS if k == 0 or with_phi else 1)
+                prepare(k, BLOCK_BANKS if k == 0 else BLOCK_BANKS - 1 if with_phi else 1)
                 if with_phi:
                     basis(units_done)
                     units_done += 1

@@ -41,8 +41,22 @@ BLOCK_PASSES = PASSES_2 // SWEEPS
 BLOCK_BANKS = BLOCK_WORDS // BANK
 
 RUN = 2
+PACKED = 8
+LAG = 2
+REGROUP = 3
+EARLY_CHUNKS = 2
+EARLY_BLOCKS = 0
+V_ALL = 1
+VB_PHI = 3
+CATCH = 2
+SINGLES = 6
+TAIL = 2
+TAIL_V = (2, 5)
+M28 = 1
+M29 = 3
+M30 = 7
 STREAM_BUFS = 8
-PHI_EVERY = TILES // (UNITS // SWEEPS)
+PHI_EVERY = 4
 
 FLOPS = 2 * PIX * C_IN * HID + 2 * PIX * HID * KNOTS * C_OUT
 
@@ -56,8 +70,8 @@ def tile_rbfkanhead_w_kernel(
         stream = ctx.enter_context(tc.tile_pool(name="stream", bufs=STREAM_BUFS))
         twice = ctx.enter_context(tc.tile_pool(name="twice", bufs=HID_CHUNKS))
         work = ctx.enter_context(tc.tile_pool(name="work", bufs=2))
-        regroup = ctx.enter_context(tc.tile_pool(name="regroup", bufs=2 * RUN))
-        packed = ctx.enter_context(tc.tile_pool(name="packed", bufs=3 * RUN))
+        regroup = ctx.enter_context(tc.tile_pool(name="regroup", bufs=REGROUP))
+        packed = ctx.enter_context(tc.tile_pool(name="packed", bufs=PACKED))
         banks = ctx.enter_context(tc.psum_pool(name="banks", bufs=7))
         sums = ctx.enter_context(tc.psum_pool(name="sums", bufs=1))
         ctx.enter_context(tc.manual_schedule())
@@ -82,10 +96,14 @@ def tile_rbfkanhead_w_kernel(
             weight_block[k] = stream.tile(
                 [P, BLOCK_WORDS], F32, name="weight_block%d" % k, tag="stream", align_bytes=64
             )
-            nc.sync.dma_start(
-                out=weight_block[k][:].bitcast(BF16),
-                in_=out_weight[rows, chans, :].rearrange("o c k -> o (c k)"),
-            )
+            pieces = BLOCK_BANKS if k >= BLOCKS - TAIL else 1
+            row = out_weight[rows, chans, :].rearrange("o c k -> o (c k)")
+            n = 2 * BLOCK_WORDS // pieces
+            for i in range(pieces):
+                nc.sync.dma_start(
+                    out=weight_block[k][:].bitcast(BF16)[:, i * n : (i + 1) * n],
+                    in_=row[:, i * n : (i + 1) * n],
+                )
 
         x_rows = keep.tile([P, BATCH, PASSES_1, PACK, HW], BF16)
         for b in range(BATCH):
@@ -102,10 +120,22 @@ def tile_rbfkanhead_w_kernel(
                 in_=w_in_scales[:, 4 * quarter : 4 * quarter + 4, :].bitcast(I32),
             )
 
-        for j in range(HID_CHUNKS):
-            load_w_in_chunk(j)
-        for k in range(STREAM_BUFS - HID_CHUNKS):
-            load_weight_block(k)
+        stream_order = (
+            [(load_w_in_chunk, j) for j in range(EARLY_CHUNKS)]
+            + [(load_weight_block, k) for k in range(EARLY_BLOCKS)]
+            + [(load_w_in_chunk, j) for j in range(EARLY_CHUNKS, HID_CHUNKS)]
+            + [(load_weight_block, k) for k in range(EARLY_BLOCKS, BLOCKS)]
+        )
+        issued = [0]
+
+        def load_next():
+            if issued[0] < len(stream_order):
+                load, n = stream_order[issued[0]]
+                issued[0] += 1
+                load(n)
+
+        for n in range(STREAM_BUFS):
+            load_next()
 
         square = keep.tile([P, P], F32)
         nc.vector.memset(square[:], 0.0)
@@ -196,7 +226,7 @@ def tile_rbfkanhead_w_kernel(
                 out=z_twice[j][:].rearrange("x (c d) -> x c d", d=2),
                 in_=z_bank[:].unsqueeze(2).to_broadcast([P, HID_CHUNK, 2]),
             )
-            load_weight_block(STREAM_BUFS - HID_CHUNKS + j)
+            load_next()
 
         def basis(n):
             j, part = divmod(n, CHUNK_UNITS)
@@ -239,41 +269,44 @@ def tile_rbfkanhead_w_kernel(
         sum_bank = sums.tile([P, PER_BANK, PIX], F32)
         result = keep.tile([P, TILES, PIX], F32)
 
-        def quantise_weight(k, pieces):
-            weight_codes[k] = packed.tile([P, BLOCK_PASSES * P], U32, name="weight_codes", align_bytes=64)
-            weight_planes[k] = packed.tile([P, BLOCK_PASSES * P], U8, name="weight_planes", align_bytes=64)
-            for n in range(pieces):
-                words = slice(n * BLOCK_PASSES * P // pieces, (n + 1) * BLOCK_PASSES * P // pieces)
-                pairs = slice(n * BLOCK_WORDS // pieces, (n + 1) * BLOCK_WORDS // pieces)
-                nc.vector.quantize_mx(
-                    out=weight_codes[k][:, words].bitcast(FP8X4),
-                    scales=weight_planes[k][:, words],
-                    in_=grouped[k][:, pairs].bitcast(BF16),
+        def quantise_weight(k, pieces=1, n=0):
+            if n == 0:
+                weight_codes[k] = packed.tile([P, BLOCK_PASSES * P], U32, name="weight_codes", align_bytes=64)
+                weight_planes[k] = packed.tile([P, BLOCK_PASSES * P], U8, name="weight_planes", align_bytes=64)
+            words = slice(n * BLOCK_PASSES * P // pieces, (n + 1) * BLOCK_PASSES * P // pieces)
+            pairs = slice(n * BLOCK_WORDS // pieces, (n + 1) * BLOCK_WORDS // pieces)
+            nc.vector.quantize_mx(
+                out=weight_codes[k][:, words].bitcast(FP8X4),
+                scales=weight_planes[k][:, words],
+                in_=grouped[k][:, pairs].bitcast(BF16),
+            )
+
+        def fill_bank(k, b, on_vector):
+            if b == 0:
+                grouped[k] = regroup.tile([P, BLOCK_WORDS], F32, name="grouped", align_bytes=64)
+            w_t = banks.tile([P, 2, 2, P], F32, name="w_t", tag="bank")
+            for m in range(PER_BANK):
+                n = b * PER_BANK + m
+                nc.tensor.transpose(
+                    w_t[:, m // 2, m % 2, :], weight_block[k][:, n * P : (n + 1) * P], ident[:]
                 )
+            dst = grouped[k][:, b * BANK : (b + 1) * BANK].rearrange("p (g o u) -> p g o u", g=2, u=2)
+            src = w_t[:].rearrange("p g u o -> p g o u")
+            if on_vector:
+                nc.vector.tensor_copy(out=dst, in_=src)
+            else:
+                nc.scalar.copy(out=dst, in_=src)
 
         def prepare(k, vector_banks):
-            grouped[k] = regroup.tile([P, BLOCK_WORDS], F32, name="grouped", align_bytes=64)
             for b in range(BLOCK_BANKS):
-                w_t = banks.tile([P, 2, 2, P], F32, name="w_t", tag="bank")
-                for m in range(PER_BANK):
-                    n = b * PER_BANK + m
-                    nc.tensor.transpose(
-                        w_t[:, m // 2, m % 2, :], weight_block[k][:, n * P : (n + 1) * P], ident[:]
-                    )
-                dst = grouped[k][:, b * BANK : (b + 1) * BANK].rearrange("p (g o u) -> p g o u", g=2, u=2)
-                src = w_t[:].rearrange("p g u o -> p g o u")
-                if b < vector_banks:
-                    nc.vector.tensor_copy(out=dst, in_=src)
-                else:
-                    nc.scalar.copy(out=dst, in_=src)
+                fill_bank(k, b, b < vector_banks)
                 if b == 0 and k > 0:
-                    quantise_weight(k - 1, 1)
-            if k + STREAM_BUFS < BLOCKS:
-                load_weight_block(k + STREAM_BUFS)
+                    quantise_weight(k - 1)
+            load_next()
 
-        def multiply(k):
+        def multiply(k, passes=range(BLOCK_PASSES)):
             first_pass = (k // TILES) * BLOCK_PASSES
-            for g in range(BLOCK_PASSES):
+            for g in passes:
                 cols = slice(g * P, (g + 1) * P)
                 pixels = slice((first_pass + g) * PIX, (first_pass + g + 1) * PIX)
                 nc.tensor.matmul_mx(
@@ -309,43 +342,80 @@ def tile_rbfkanhead_w_kernel(
                 in_=result[:, tile_i, :].rearrange("o (b x) -> o b x", b=BATCH),
             )
 
-        for j in range(HID_CHUNKS):
+        for j in range(EARLY_CHUNKS):
             first_product(j)
-            if j < HID_CHUNKS // SWEEPS:
-                for n in range(j * CHUNK_UNITS, (j + 1) * CHUNK_UNITS):
-                    basis(n)
-
-        units_done = UNITS // SWEEPS
+            for n in range(j * CHUNK_UNITS, (j + 1) * CHUNK_UNITS):
+                basis(n)
+        units_done = EARLY_CHUNKS * CHUNK_UNITS
         chunks_done = 0
         stored = 0
-        for first in range(0, BLOCKS, RUN):
-            for k in range(max(first - 2 * RUN, 0), max(first - RUN, 0)):
+        singles_from = BLOCKS - TAIL - SINGLES
+        starts = list(range(0, singles_from, RUN)) + list(range(singles_from, BLOCKS - TAIL))
+        multiplied = 0
+        collected = 0
+        for first in starts:
+            run = RUN if first < singles_from else 1
+            if first == EARLY_BLOCKS:
+                for j in range(EARLY_CHUNKS, HID_CHUNKS):
+                    first_product(j)
+                    if j < HID_CHUNKS // SWEEPS:
+                        for n in range(j * CHUNK_UNITS, (j + 1) * CHUNK_UNITS):
+                            basis(n)
+                        units_done += CHUNK_UNITS
+            for k in range(collected, multiplied):
                 collect(k)
+            collected = multiplied
             chunks_ready = units_done // CHUNK_UNITS
-            for k in range(first, first + RUN):
-                with_phi = k < TILES and k % PHI_EVERY == PHI_EVERY - 1
-                prepare(k, BLOCK_BANKS if k == 0 else BLOCK_BANKS - 1 if with_phi else 1)
+            for k in range(first, first + run):
+                with_phi = units_done < UNITS and k % PHI_EVERY == PHI_EVERY - 1
+                prepare(k, BLOCK_BANKS if k < V_ALL else VB_PHI if with_phi else 1)
                 if with_phi:
                     basis(units_done)
                     units_done += 1
             for j in range(chunks_done, chunks_ready):
                 quantise_phi(j)
             chunks_done = chunks_ready
-            for k in range(max(first - RUN, 0), first):
+            due = max(first + run - LAG, 0)
+            if chunks_done < HID_CHUNKS // SWEEPS:
+                due = 0
+            due = min(due, multiplied + run + CATCH)
+            for k in range(multiplied, due):
                 multiply(k)
-            if first + RUN + STREAM_BUFS >= BLOCKS:
-                for tile_i in range(stored, max(first - 2 * RUN - TILES, 0)):
+            multiplied = due
+            if issued[0] == len(stream_order):
+                for tile_i in range(stored, max(collected - TILES, 0)):
                     store(tile_i)
-                stored = max(first - 2 * RUN - TILES, stored)
+                stored = max(collected - TILES, stored)
 
-        quantise_weight(BLOCKS - 1, BLOCK_BANKS)
-        for k in range(BLOCKS - 2 * RUN, BLOCKS - RUN):
+        while multiplied < BLOCKS - TAIL - 2:
+            multiply(multiplied)
+            multiplied += 1
+        for k in range(collected, multiplied):
             collect(k)
-        for tile_i in range(stored, TILES - RUN):
-            store(tile_i)
-        for k in range(BLOCKS - RUN, BLOCKS):
-            multiply(k)
-        for k in range(BLOCKS - RUN, BLOCKS):
+        collected = multiplied
+        for i in range(TAIL * BLOCK_BANKS):
+            k = BLOCKS - TAIL + i // BLOCK_BANKS
+            fill_bank(k, i % BLOCK_BANKS, i in TAIL_V)
+            if i == 0:
+                quantise_weight(BLOCKS - TAIL - 1)
+            else:
+                quantise_weight(BLOCKS - TAIL + (i - 1) // BLOCK_BANKS, BLOCK_BANKS, (i - 1) % BLOCK_BANKS)
+            if i in (M28, M29):
+                multiply(multiplied)
+                multiplied += 1
+            if i == M29:
+                for j in range(collected, multiplied):
+                    collect(j)
+                for tile_i in range(stored, multiplied - TILES):
+                    store(tile_i)
+            if i == M30:
+                multiply(BLOCKS - 2)
+        if M30 > 7:
+            multiply(BLOCKS - 2)
+        multiply(BLOCKS - 1, range(0, BLOCK_PASSES - 2))
+        quantise_weight(BLOCKS - 1, BLOCK_BANKS, BLOCK_BANKS - 1)
+        multiply(BLOCKS - 1, range(BLOCK_PASSES - 2, BLOCK_PASSES))
+        for k in range(BLOCKS - TAIL, BLOCKS):
             collect(k)
-        for tile_i in range(TILES - RUN, TILES):
+        for tile_i in range(TILES - TAIL, TILES):
             store(tile_i)

@@ -41,6 +41,12 @@ BLOCK_PASSES = PASSES_2 // SWEEPS
 BLOCK_BANKS = BLOCK_WORDS // BANK
 
 RUN = 2
+PLANE_CUT = 2048
+HEAD = [('f', 0), ('b', 0), ('f', 1), ('b', 1), ('f', 2), ('b', 2), ('f', 3), ('b', 3)]
+EXTRA = ()
+VBS = {0: 4, 1: 2}
+VPAT = (1, 1, 1, 0)
+QAT = 0
 PACKED = 8
 LAG = 2
 REGROUP = 3
@@ -49,14 +55,14 @@ EARLY_BLOCKS = 0
 V_ALL = 1
 VB_PHI = 3
 CATCH = 2
-SINGLES = 6
+SINGLES = 0
 TAIL = 2
-TAIL_V = (2, 5)
-M28 = 1
-M29 = 3
+TAIL_V = (2,)
+M28 = 3
 M30 = 7
 STREAM_BUFS = 8
 PHI_EVERY = 4
+PHI_FROM = 0
 
 FLOPS = 2 * PIX * C_IN * HID + 2 * PIX * HID * KNOTS * C_OUT
 
@@ -114,18 +120,20 @@ def tile_rbfkanhead_w_kernel(
 
         w_in_planes = keep.tile([P, HID], U8, align_bytes=64)
         nc.vector.memset(w_in_planes[:].bitcast(I32), 0)
-        for quarter in range(4):
-            nc.sync.dma_start(
-                out=w_in_planes[32 * quarter : 32 * quarter + 16, :].bitcast(I32),
-                in_=w_in_scales[:, 4 * quarter : 4 * quarter + 4, :].bitcast(I32),
-            )
 
-        stream_order = (
-            [(load_w_in_chunk, j) for j in range(EARLY_CHUNKS)]
-            + [(load_weight_block, k) for k in range(EARLY_BLOCKS)]
-            + [(load_w_in_chunk, j) for j in range(EARLY_CHUNKS, HID_CHUNKS)]
-            + [(load_weight_block, k) for k in range(EARLY_BLOCKS, BLOCKS)]
-        )
+        def load_planes(cols):
+            for quarter in range(4):
+                nc.sync.dma_start(
+                    out=w_in_planes[32 * quarter : 32 * quarter + 16, cols].bitcast(I32),
+                    in_=w_in_scales[:, 4 * quarter : 4 * quarter + 4, cols].bitcast(I32),
+                )
+
+        load_planes(slice(0, PLANE_CUT))
+
+        if PLANE_CUT < HID:
+            load_w_in_chunk(0)
+            load_planes(slice(PLANE_CUT, HID))
+        stream_order = [(load_w_in_chunk, j) for j in range(1 if PLANE_CUT < HID else 0, HID_CHUNKS)] + [(load_weight_block, k) for k in range(BLOCKS)]
         issued = [0]
 
         def load_next():
@@ -134,7 +142,7 @@ def tile_rbfkanhead_w_kernel(
                 issued[0] += 1
                 load(n)
 
-        for n in range(STREAM_BUFS):
+        for n in range(STREAM_BUFS - (1 if PLANE_CUT < HID else 0)):
             load_next()
 
         square = keep.tile([P, P], F32)
@@ -151,6 +159,20 @@ def tile_rbfkanhead_w_kernel(
         )
         nc.scalar.dma_start(out=b_in_rows[64:96, :], in_=b_in.rearrange("(s c) -> s c", s=SLABS))
         nc.scalar.dma_start(out=out_bias_rows[96:112, :], in_=out_bias.rearrange("(i o) -> i o", i=TILES))
+        x_grouped = keep.tile([P, PASSES_1, PIX, PACK], BF16, align_bytes=64)
+        for b in range(BATCH):
+            nc.vector.tensor_copy(
+                out=x_grouped[:, :, b * HW : (b + 1) * HW, :],
+                in_=x_rows[:, b].rearrange("p g t x -> p g x t"),
+            )
+        x_codes = keep.tile([P, PASSES_1 * PIX], U32, align_bytes=64)
+        x_planes = keep.tile([P, PASSES_1 * PIX], U8, align_bytes=64)
+        nc.vector.quantize_mx(
+            out=x_codes[:].bitcast(FP8X4),
+            scales=x_planes[:],
+            in_=x_grouped[:].rearrange("p g x t -> p (g x t)"),
+        )
+
         nc.vector.tensor_copy(
             out=square[64:96, :].rearrange("s (c d) -> s c d", d=2),
             in_=b_in_rows[64:96, :].unsqueeze(2).to_broadcast([32, SLAB_CH, 2]),
@@ -167,20 +189,6 @@ def tile_rbfkanhead_w_kernel(
         log_widths_col = columns[:, 32:64].bitcast(BF16)
         b_in_col = columns[:, 64:96]
         out_bias_col = columns[:, 96:112]
-
-        x_grouped = keep.tile([P, PASSES_1, PIX, PACK], BF16, align_bytes=64)
-        for b in range(BATCH):
-            nc.vector.tensor_copy(
-                out=x_grouped[:, :, b * HW : (b + 1) * HW, :],
-                in_=x_rows[:, b].rearrange("p g t x -> p g x t"),
-            )
-        x_codes = keep.tile([P, PASSES_1 * PIX], U32, align_bytes=64)
-        x_planes = keep.tile([P, PASSES_1 * PIX], U8, align_bytes=64)
-        nc.vector.quantize_mx(
-            out=x_codes[:].bitcast(FP8X4),
-            scales=x_planes[:],
-            in_=x_grouped[:].rearrange("p g x t -> p (g x t)"),
-        )
 
         soft = keep.tile([P, 2 * SLABS], F32)
         nc.scalar.activation(out=soft[:], in_=log_widths_col, func=ACT.Abs)
@@ -300,7 +308,7 @@ def tile_rbfkanhead_w_kernel(
         def prepare(k, vector_banks):
             for b in range(BLOCK_BANKS):
                 fill_bank(k, b, b < vector_banks)
-                if b == 0 and k > 0:
+                if b == (0 if vector_banks else QAT) and k > 0:
                     quantise_weight(k - 1)
             load_next()
 
@@ -342,11 +350,13 @@ def tile_rbfkanhead_w_kernel(
                 in_=result[:, tile_i, :].rearrange("o (b x) -> o b x", b=BATCH),
             )
 
-        for j in range(EARLY_CHUNKS):
-            first_product(j)
-            for n in range(j * CHUNK_UNITS, (j + 1) * CHUNK_UNITS):
+        units_done = 0
+        for what, n in HEAD:
+            if what == "f":
+                first_product(n)
+            else:
                 basis(n)
-        units_done = EARLY_CHUNKS * CHUNK_UNITS
+                units_done += 1
         chunks_done = 0
         stored = 0
         singles_from = BLOCKS - TAIL - SINGLES
@@ -355,21 +365,14 @@ def tile_rbfkanhead_w_kernel(
         collected = 0
         for first in starts:
             run = RUN if first < singles_from else 1
-            if first == EARLY_BLOCKS:
-                for j in range(EARLY_CHUNKS, HID_CHUNKS):
-                    first_product(j)
-                    if j < HID_CHUNKS // SWEEPS:
-                        for n in range(j * CHUNK_UNITS, (j + 1) * CHUNK_UNITS):
-                            basis(n)
-                        units_done += CHUNK_UNITS
             for k in range(collected, multiplied):
                 collect(k)
             collected = multiplied
             chunks_ready = units_done // CHUNK_UNITS
             for k in range(first, first + run):
-                with_phi = units_done < UNITS and k % PHI_EVERY == PHI_EVERY - 1
-                prepare(k, BLOCK_BANKS if k < V_ALL else VB_PHI if with_phi else 1)
-                if with_phi:
+                with_phi = units_done < UNITS and k >= PHI_FROM and k % PHI_EVERY == PHI_EVERY - 1
+                prepare(k, VBS.get(k, VB_PHI if with_phi else VPAT[k % len(VPAT)]))
+                if with_phi or k in EXTRA:
                     basis(units_done)
                     units_done += 1
             for j in range(chunks_done, chunks_ready):
@@ -400,10 +403,10 @@ def tile_rbfkanhead_w_kernel(
                 quantise_weight(BLOCKS - TAIL - 1)
             else:
                 quantise_weight(BLOCKS - TAIL + (i - 1) // BLOCK_BANKS, BLOCK_BANKS, (i - 1) % BLOCK_BANKS)
-            if i in (M28, M29):
-                multiply(multiplied)
-                multiplied += 1
-            if i == M29:
+            if i == M28:
+                while multiplied < BLOCKS - TAIL:
+                    multiply(multiplied)
+                    multiplied += 1
                 for j in range(collected, multiplied):
                     collect(j)
                 for tile_i in range(stored, multiplied - TILES):

@@ -41,10 +41,13 @@ BLOCK_PASSES = PASSES_2 // SWEEPS
 BLOCK_BANKS = BLOCK_WORDS // BANK
 
 RUN = 2
-PLANE_CUT = 2048
+EARLY_TO = 4
+WPIECES = 1
+ZPIECES = 2
+PLANE_CUT = 512
 HEAD = [('f', 0), ('b', 0), ('f', 1), ('b', 1), ('f', 2), ('b', 2), ('f', 3), ('b', 3)]
 EXTRA = ()
-VBS = {0: 4, 1: 2}
+VBS = {0: 4, 1: 1}
 VPAT = (1, 1, 1, 0)
 QAT = 0
 PACKED = 8
@@ -55,10 +58,11 @@ EARLY_BLOCKS = 0
 V_ALL = 1
 VB_PHI = 3
 CATCH = 2
-SINGLES = 0
+SINGLES = 2
 TAIL = 2
-TAIL_V = (2,)
+TAIL_V = (2, 5)
 M28 = 3
+M29 = 3
 M30 = 7
 STREAM_BUFS = 8
 PHI_EVERY = 4
@@ -90,10 +94,14 @@ def tile_rbfkanhead_w_kernel(
             w_in_chunk[j] = stream.tile(
                 [P, PASSES_1, HID_CHUNK], I32, name="w_in_chunk%d" % j, tag="stream", align_bytes=64
             )
-            nc.sync.dma_start(
-                out=w_in_chunk[j][:],
-                in_=w_in_words[:, :, cols, :].rearrange("g p n t -> p g (n t)").bitcast(I32),
-            )
+            pieces = WPIECES if j == 0 else 1
+            n = HID_CHUNK // pieces
+            for i in range(pieces):
+                cols = slice(j * HID_CHUNK + i * n, j * HID_CHUNK + (i + 1) * n)
+                nc.sync.dma_start(
+                    out=w_in_chunk[j][:, :, i * n : (i + 1) * n],
+                    in_=w_in_words[:, :, cols, :].rearrange("g p n t -> p g (n t)").bitcast(I32),
+                )
 
         def load_weight_block(k):
             sweep, tile_i = divmod(k, TILES)
@@ -217,23 +225,29 @@ def tile_rbfkanhead_w_kernel(
         phi_planes = keep.tile([P, PASSES_2 * PIX], U8, align_bytes=64)
 
         def first_product(j):
-            cols = slice(j * HID_CHUNK, (j + 1) * HID_CHUNK)
-            z_bank = banks.tile([P, BANK], F32, name="z_bank", tag="bank")
-            for g in range(PASSES_1):
-                nc.tensor.matmul_mx(
-                    out=z_bank[:],
-                    lhsT=x_codes[:, g * PIX : (g + 1) * PIX].bitcast(FP8X4),
-                    lhsT_scale=x_planes[:, g * PIX : (g + 1) * PIX],
-                    rhs=w_in_chunk[j][:, g, :].bitcast(FP8X4),
-                    rhs_scale=w_in_planes[4 * g : P, cols],
-                    start=(g == 0),
-                    stop=(g == PASSES_1 - 1),
-                )
+            pieces = WPIECES if j == 0 else 1
+            copies = max(pieces, ZPIECES if j == 0 else 1) // pieces
+            n = HID_CHUNK // pieces
             z_twice[j] = twice.tile([P, 2 * HID_CHUNK], F32, name="z_twice")
-            nc.vector.tensor_copy(
-                out=z_twice[j][:].rearrange("x (c d) -> x c d", d=2),
-                in_=z_bank[:].unsqueeze(2).to_broadcast([P, HID_CHUNK, 2]),
-            )
+            for i in range(pieces):
+                z_bank = banks.tile([P, BANK], F32, name="z_bank", tag="bank")
+                cols = slice(j * HID_CHUNK + i * n, j * HID_CHUNK + (i + 1) * n)
+                for g in range(PASSES_1):
+                    nc.tensor.matmul_mx(
+                        out=z_bank[:, 0:n],
+                        lhsT=x_codes[:, g * PIX : (g + 1) * PIX].bitcast(FP8X4),
+                        lhsT_scale=x_planes[:, g * PIX : (g + 1) * PIX],
+                        rhs=w_in_chunk[j][:, g, i * n : (i + 1) * n].bitcast(FP8X4),
+                        rhs_scale=w_in_planes[4 * g : P, cols],
+                        start=(g == 0),
+                        stop=(g == PASSES_1 - 1),
+                    )
+                m = n // copies
+                for c in range(copies):
+                    nc.vector.tensor_copy(
+                        out=z_twice[j][:, 2 * (i * n + c * m) : 2 * (i * n + (c + 1) * m)].rearrange("x (c d) -> x c d", d=2),
+                        in_=z_bank[:, c * m : (c + 1) * m].unsqueeze(2).to_broadcast([P, m, 2]),
+                    )
             load_next()
 
         def basis(n):
@@ -360,11 +374,13 @@ def tile_rbfkanhead_w_kernel(
         chunks_done = 0
         stored = 0
         singles_from = BLOCKS - TAIL - SINGLES
-        starts = list(range(0, singles_from, RUN)) + list(range(singles_from, BLOCKS - TAIL))
+        starts = [0] + list(range(RUN, EARLY_TO)) + list(range(EARLY_TO, singles_from, RUN)) + list(range(singles_from, BLOCKS - TAIL))
+        starts.append(BLOCKS - TAIL)
         multiplied = 0
         collected = 0
-        for first in starts:
-            run = RUN if first < singles_from else 1
+        for step in range(len(starts) - 1):
+            first = starts[step]
+            run = starts[step + 1] - first
             for k in range(collected, multiplied):
                 collect(k)
             collected = multiplied
@@ -403,7 +419,10 @@ def tile_rbfkanhead_w_kernel(
                 quantise_weight(BLOCKS - TAIL - 1)
             else:
                 quantise_weight(BLOCKS - TAIL + (i - 1) // BLOCK_BANKS, BLOCK_BANKS, (i - 1) % BLOCK_BANKS)
-            if i == M28:
+            if i == M28 and M28 < M29:
+                multiply(multiplied)
+                multiplied += 1
+            if i == M29:
                 while multiplied < BLOCKS - TAIL:
                     multiply(multiplied)
                     multiplied += 1

from contextlib import ExitStack

import concourse.mybir as mybir
from concourse.masks import make_identity

F32 = mybir.dt.float32
BF16 = mybir.dt.bfloat16
I32 = mybir.dt.int32
U32 = mybir.dt.uint32
U8 = mybir.dt.uint8
FP8X4 = mybir.dt.float8_e4m3fn_x4
ACT = mybir.ActivationFunctionType
ALU = mybir.AluOpType

BATCH, C_IN, HW, HID, KNOTS, C_OUT = 2, 2048, 64, 2048, 4, 2048
PIX = BATCH * HW

P = 128
PACK = 4
K_PASS = P * PACK
BANK = 512
PER_BANK = BANK // P

PASSES_1 = C_IN // K_PASS
PASSES_2 = HID * KNOTS // K_PASS
SLABS = 2 * PASSES_2
SLAB_CH = HID // SLABS

HID_CHUNK = BANK
HID_CHUNKS = HID // HID_CHUNK
CHUNK_PASSES = PASSES_2 // HID_CHUNKS
UNITS = SLABS // PER_BANK
UNIT_PASSES = PASSES_2 // UNITS
CHUNK_UNITS = UNITS // HID_CHUNKS

TILES = C_OUT // P
SWEEPS = 2
BLOCKS = SWEEPS * TILES
BLOCK_WORDS = HID * KNOTS // 2 // SWEEPS
BLOCK_PASSES = PASSES_2 // SWEEPS
BLOCK_BANKS = BLOCK_WORDS // BANK

RUN = 2
EARLY_TO = 4
WPIECES = 1
ZPIECES = 2
PLANE_CUT = 512
HEAD = [('f', 0), ('b', 0), ('f', 1), ('b', 1), ('f', 2), ('b', 2), ('f', 3), ('b', 3)]
EXTRA = ()
VBS = {0: 4, 1: 1}
VPAT = (1, 1, 1, 0)
QAT = 0
PACKED = 8
LAG = 2
REGROUP = 3
EARLY_CHUNKS = 2
EARLY_BLOCKS = 0
V_ALL = 1
VB_PHI = 3
CATCH = 2
SINGLES = 2
TAIL = 2
TAIL_V = (2, 5)
M28 = 3
M29 = 3
M30 = 7
STREAM_BUFS = 8
PHI_EVERY = 4
PHI_FROM = 0

FLOPS = 2 * PIX * C_IN * HID + 2 * PIX * HID * KNOTS * C_OUT


def tile_rbfkanhead_w_kernel(
    tc, x, w_in_words, w_in_scales, b_in, centers, log_widths, out_weight, out_bias, out
):
    nc = tc.nc
    with ExitStack() as ctx:
        keep = ctx.enter_context(tc.tile_pool(name="keep", bufs=1))
        stream = ctx.enter_context(tc.tile_pool(name="stream", bufs=STREAM_BUFS))
        twice = ctx.enter_context(tc.tile_pool(name="twice", bufs=HID_CHUNKS))
        work = ctx.enter_context(tc.tile_pool(name="work", bufs=2))
        regroup = ctx.enter_context(tc.tile_pool(name="regroup", bufs=REGROUP))
        packed = ctx.enter_context(tc.tile_pool(name="packed", bufs=PACKED))
        banks = ctx.enter_context(tc.psum_pool(name="banks", bufs=7))
        sums = ctx.enter_context(tc.psum_pool(name="sums", bufs=1))
        ctx.enter_context(tc.manual_schedule())

        w_in_chunk = {}
        weight_block = {}

        def load_w_in_chunk(j):
            cols = slice(j * HID_CHUNK, (j + 1) * HID_CHUNK)
            w_in_chunk[j] = stream.tile(
                [P, PASSES_1, HID_CHUNK], I32, name="w_in_chunk%d" % j, tag="stream", align_bytes=64
            )
            pieces = WPIECES if j == 0 else 1
            n = HID_CHUNK // pieces
            for i in range(pieces):
                cols = slice(j * HID_CHUNK + i * n, j * HID_CHUNK + (i + 1) * n)
                nc.sync.dma_start(
                    out=w_in_chunk[j][:, :, i * n : (i + 1) * n],
                    in_=w_in_words[:, :, cols, :].rearrange("g p n t -> p g (n t)").bitcast(I32),
                )

        def load_weight_block(k):
            sweep, tile_i = divmod(k, TILES)
            rows = slice(tile_i * P, (tile_i + 1) * P)
            chans = slice(sweep * (HID // SWEEPS), (sweep + 1) * (HID // SWEEPS))
            weight_block[k] = stream.tile(
                [P, BLOCK_WORDS], F32, name="weight_block%d" % k, tag="stream", align_bytes=64
            )
            pieces = BLOCK_BANKS if k >= BLOCKS - TAIL else 1
            row = out_weight[rows, chans, :].rearrange("o c k -> o (c k)")
            n = 2 * BLOCK_WORDS // pieces
            for i in range(pieces):
                nc.sync.dma_start(
                    out=weight_block[k][:].bitcast(BF16)[:, i * n : (i + 1) * n],
                    in_=row[:, i * n : (i + 1) * n],
                )

        x_rows = keep.tile([P, BATCH, PASSES_1, PACK, HW], BF16)
        for b in range(BATCH):
            nc.sync.dma_start(
                out=x_rows[:, b].rearrange("p g t x -> p g (t x)"),
                in_=x[b].rearrange("(g p t) h w -> p g (t h w)", g=PASSES_1, p=P, t=PACK),
            )

        w_in_planes = keep.tile([P, HID], U8, align_bytes=64)
        nc.vector.memset(w_in_planes[:].bitcast(I32), 0)

        def load_planes(cols):
            for quarter in range(4):
                nc.sync.dma_start(
                    out=w_in_planes[32 * quarter : 32 * quarter + 16, cols].bitcast(I32),
                    in_=w_in_scales[:, 4 * quarter : 4 * quarter + 4, cols].bitcast(I32),
                )

        load_planes(slice(0, PLANE_CUT))

        if PLANE_CUT < HID:
            load_w_in_chunk(0)
            load_planes(slice(PLANE_CUT, HID))
        stream_order = [(load_w_in_chunk, j) for j in range(1 if PLANE_CUT < HID else 0, HID_CHUNKS)] + [(load_weight_block, k) for k in range(BLOCKS)]
        issued = [0]

        def load_next():
            if issued[0] < len(stream_order):
                load, n = stream_order[issued[0]]
                issued[0] += 1
                load(n)

        for n in range(STREAM_BUFS - (1 if PLANE_CUT < HID else 0)):
            load_next()

        square = keep.tile([P, P], F32)
        nc.vector.memset(square[:], 0.0)
        b_in_rows = keep.tile([P, SLAB_CH], BF16)
        out_bias_rows = keep.tile([P, P], BF16)
        nc.scalar.dma_start(
            out=square[0:32, :].bitcast(BF16),
            in_=centers.rearrange("a (s c) k h w -> (a s) (c k h w)", s=SLABS),
        )
        nc.scalar.dma_start(
            out=square[32:64, :].bitcast(BF16),
            in_=log_widths.rearrange("a (s c) k h w -> (a s) (c k h w)", s=SLABS),
        )
        nc.scalar.dma_start(out=b_in_rows[64:96, :], in_=b_in.rearrange("(s c) -> s c", s=SLABS))
        nc.scalar.dma_start(out=out_bias_rows[96:112, :], in_=out_bias.rearrange("(i o) -> i o", i=TILES))
        x_grouped = keep.tile([P, PASSES_1, PIX, PACK], BF16, align_bytes=64)
        for b in range(BATCH):
            nc.vector.tensor_copy(
                out=x_grouped[:, :, b * HW : (b + 1) * HW, :],
                in_=x_rows[:, b].rearrange("p g t x -> p g x t"),
            )
        x_codes = keep.tile([P, PASSES_1 * PIX], U32, align_bytes=64)
        x_planes = keep.tile([P, PASSES_1 * PIX], U8, align_bytes=64)
        nc.vector.quantize_mx(
            out=x_codes[:].bitcast(FP8X4),
            scales=x_planes[:],
            in_=x_grouped[:].rearrange("p g x t -> p (g x t)"),
        )

        nc.vector.tensor_copy(
            out=square[64:96, :].rearrange("s (c d) -> s c d", d=2),
            in_=b_in_rows[64:96, :].unsqueeze(2).to_broadcast([32, SLAB_CH, 2]),
        )
        nc.vector.tensor_copy(out=square[96:112, :], in_=out_bias_rows[96:112, :])

        ident = keep.tile([P, P], F32)
        make_identity(nc, ident[:])
        square_t = banks.tile([P, BANK], F32, name="square_t", tag="bank")
        nc.tensor.transpose(square_t[:, 0:P], square[:], ident[:])
        columns = keep.tile([P, P], F32)
        nc.vector.tensor_copy(out=columns[:], in_=square_t[:, 0:P])
        centers_col = columns[:, 0:32].bitcast(BF16)
        log_widths_col = columns[:, 32:64].bitcast(BF16)
        b_in_col = columns[:, 64:96]
        out_bias_col = columns[:, 96:112]

        soft = keep.tile([P, 2 * SLABS], F32)
        nc.scalar.activation(out=soft[:], in_=log_widths_col, func=ACT.Abs)
        nc.scalar.activation(out=soft[:], in_=soft[:], func=ACT.Exp, scale=-1.0)
        nc.scalar.activation(out=soft[:], in_=soft[:], func=ACT.Ln, bias=1.0)
        exp_again = keep.tile([P, 1], F32)
        nc.scalar.activation(out=exp_again[:], in_=soft[:, 0:1], func=ACT.Exp)
        width = keep.tile([P, 2 * SLABS], F32)
        nc.vector.tensor_scalar(out=width[:], in0=log_widths_col, scalar1=0.0, scalar2=None, op0=ALU.max)
        nc.vector.tensor_tensor(out=width[:], in0=width[:], in1=soft[:], op=ALU.add)
        nc.vector.tensor_scalar(out=width[:], in0=width[:], scalar1=1e-4, scalar2=None, op0=ALU.add)
        inv_width = keep.tile([P, 2 * SLABS], F32)
        nc.vector.reciprocal(out=inv_width[:], in_=width[:])
        offset = keep.tile([P, 2 * SLABS], F32)
        nc.vector.tensor_tensor(
            out=offset[:].rearrange("p (s e) -> p s e", e=2),
            in0=b_in_col.unsqueeze(2).to_broadcast([P, SLABS, 2]),
            in1=centers_col.rearrange("p (s e) -> p s e", e=2),
            op=ALU.subtract,
        )
        nc.vector.tensor_tensor(out=offset[:], in0=offset[:], in1=inv_width[:], op=ALU.mult)

        z_twice = {}
        phi = keep.tile([P, PASSES_2, PIX, PACK], BF16, align_bytes=64)
        phi_codes = keep.tile([P, PASSES_2 * PIX], U32, align_bytes=64)
        phi_planes = keep.tile([P, PASSES_2 * PIX], U8, align_bytes=64)

        def first_product(j):
            pieces = WPIECES if j == 0 else 1
            copies = max(pieces, ZPIECES if j == 0 else 1) // pieces
            n = HID_CHUNK // pieces
            z_twice[j] = twice.tile([P, 2 * HID_CHUNK], F32, name="z_twice")
            for i in range(pieces):
                z_bank = banks.tile([P, BANK], F32, name="z_bank", tag="bank")
                cols = slice(j * HID_CHUNK + i * n, j * HID_CHUNK + (i + 1) * n)
                for g in range(PASSES_1):
                    nc.tensor.matmul_mx(
                        out=z_bank[:, 0:n],
                        lhsT=x_codes[:, g * PIX : (g + 1) * PIX].bitcast(FP8X4),
                        lhsT_scale=x_planes[:, g * PIX : (g + 1) * PIX],
                        rhs=w_in_chunk[j][:, g, i * n : (i + 1) * n].bitcast(FP8X4),
                        rhs_scale=w_in_planes[4 * g : P, cols],
                        start=(g == 0),
                        stop=(g == PASSES_1 - 1),
                    )
                m = n // copies
                for c in range(copies):
                    nc.vector.tensor_copy(
                        out=z_twice[j][:, 2 * (i * n + c * m) : 2 * (i * n + (c + 1) * m)].rearrange("x (c d) -> x c d", d=2),
                        in_=z_bank[:, c * m : (c + 1) * m].unsqueeze(2).to_broadcast([P, m, 2]),
                    )
            load_next()

        def basis(n):
            j, part = divmod(n, CHUNK_UNITS)
            z_t = banks.tile([P, PER_BANK, PIX], F32, name="z_t", tag="bank")
            for m in range(PER_BANK):
                col = (part * PER_BANK + m) * P
                nc.tensor.transpose(z_t[:, m, :], z_twice[j][:, col : col + P], ident[:])
            squares = work.tile([P, UNIT_PASSES, PACK, PIX], F32, name="squares")
            for m in range(PER_BANK):
                g_local, u = divmod(m, 2)
                for e in range(2):
                    col = 2 * (n * PER_BANK + m) + e
                    nc.scalar.activation(
                        out=squares[:, g_local, 2 * u + e, :],
                        in_=z_t[:, m, :],
                        func=ACT.Square,
                        scale=inv_width[:, col : col + 1],
                        bias=offset[:, col : col + 1],
                    )
            for g_local in range(UNIT_PASSES):
                nc.scalar.activation(
                    out=phi[:, n * UNIT_PASSES + g_local, :, :],
                    in_=squares[:, g_local].rearrange("p t x -> p x t"),
                    func=ACT.Exp,
                    scale=-1.0,
                )

        def quantise_phi(j):
            passes = slice(j * CHUNK_PASSES, (j + 1) * CHUNK_PASSES)
            cols = slice(j * CHUNK_PASSES * PIX, (j + 1) * CHUNK_PASSES * PIX)
            nc.vector.quantize_mx(
                out=phi_codes[:, cols].bitcast(FP8X4),
                scales=phi_planes[:, cols],
                in_=phi[:, passes].rearrange("p g x t -> p (g x t)"),
            )

        grouped = {}
        weight_codes = {}
        weight_planes = {}
        sum_bank = sums.tile([P, PER_BANK, PIX], F32)
        result = keep.tile([P, TILES, PIX], F32)

        def quantise_weight(k, pieces=1, n=0):
            if n == 0:
                weight_codes[k] = packed.tile([P, BLOCK_PASSES * P], U32, name="weight_codes", align_bytes=64)
                weight_planes[k] = packed.tile([P, BLOCK_PASSES * P], U8, name="weight_planes", align_bytes=64)
            words = slice(n * BLOCK_PASSES * P // pieces, (n + 1) * BLOCK_PASSES * P // pieces)
            pairs = slice(n * BLOCK_WORDS // pieces, (n + 1) * BLOCK_WORDS // pieces)
            nc.vector.quantize_mx(
                out=weight_codes[k][:, words].bitcast(FP8X4),
                scales=weight_planes[k][:, words],
                in_=grouped[k][:, pairs].bitcast(BF16),
            )

        def fill_bank(k, b, on_vector):
            if b == 0:
                grouped[k] = regroup.tile([P, BLOCK_WORDS], F32, name="grouped", align_bytes=64)
            w_t = banks.tile([P, 2, 2, P], F32, name="w_t", tag="bank")
            for m in range(PER_BANK):
                n = b * PER_BANK + m
                nc.tensor.transpose(
                    w_t[:, m // 2, m % 2, :], weight_block[k][:, n * P : (n + 1) * P], ident[:]
                )
            dst = grouped[k][:, b * BANK : (b + 1) * BANK].rearrange("p (g o u) -> p g o u", g=2, u=2)
            src = w_t[:].rearrange("p g u o -> p g o u")
            if on_vector:
                nc.vector.tensor_copy(out=dst, in_=src)
            else:
                nc.scalar.copy(out=dst, in_=src)

        def prepare(k, vector_banks):
            for b in range(BLOCK_BANKS):
                fill_bank(k, b, b < vector_banks)
                if b == (0 if vector_banks else QAT) and k > 0:
                    quantise_weight(k - 1)
            load_next()

        def multiply(k, passes=range(BLOCK_PASSES)):
            first_pass = (k // TILES) * BLOCK_PASSES
            for g in passes:
                cols = slice(g * P, (g + 1) * P)
                pixels = slice((first_pass + g) * PIX, (first_pass + g + 1) * PIX)
                nc.tensor.matmul_mx(
                    out=sum_bank[:, k % PER_BANK, :],
                    lhsT=weight_codes[k][:, cols].bitcast(FP8X4),
                    lhsT_scale=weight_planes[k][:, cols],
                    rhs=phi_codes[:, pixels].bitcast(FP8X4),
                    rhs_scale=phi_planes[:, pixels],
                    start=(g == 0),
                    stop=(g == BLOCK_PASSES - 1),
                )

        def collect(k):
            sweep, tile_i = divmod(k, TILES)
            if sweep == 0:
                nc.scalar.activation(
                    out=result[:, tile_i, :],
                    in_=sum_bank[:, k % PER_BANK, :],
                    func=ACT.Identity,
                    bias=out_bias_col[:, tile_i : tile_i + 1],
                )
            else:
                nc.vector.tensor_tensor(
                    out=result[:, tile_i, :],
                    in0=sum_bank[:, k % PER_BANK, :],
                    in1=result[:, tile_i, :],
                    op=ALU.add,
                )

        def store(tile_i):
            nc.sync.dma_start(
                out=out[:, tile_i * P : (tile_i + 1) * P].rearrange("b o h w -> o b (h w)"),
                in_=result[:, tile_i, :].rearrange("o (b x) -> o b x", b=BATCH),
            )

        units_done = 0
        for what, n in HEAD:
            if what == "f":
                first_product(n)
            else:
                basis(n)
                units_done += 1
        chunks_done = 0
        stored = 0
        singles_from = BLOCKS - TAIL - SINGLES
        starts = [0] + list(range(RUN, EARLY_TO)) + list(range(EARLY_TO, singles_from, RUN)) + list(range(singles_from, BLOCKS - TAIL))
        starts.append(BLOCKS - TAIL)
        multiplied = 0
        collected = 0
        for step in range(len(starts) - 1):
            first = starts[step]
            run = starts[step + 1] - first
            for k in range(collected, multiplied):
                collect(k)
            collected = multiplied
            chunks_ready = units_done // CHUNK_UNITS
            for k in range(first, first + run):
                with_phi = units_done < UNITS and k >= PHI_FROM and k % PHI_EVERY == PHI_EVERY - 1
                prepare(k, VBS.get(k, VB_PHI if with_phi else VPAT[k % len(VPAT)]))
                if with_phi or k in EXTRA:
                    basis(units_done)
                    units_done += 1
            for j in range(chunks_done, chunks_ready):
                quantise_phi(j)
            chunks_done = chunks_ready
            due = max(first + run - LAG, 0)
            if chunks_done < HID_CHUNKS // SWEEPS:
                due = 0
            due = min(due, multiplied + run + CATCH)
            for k in range(multiplied, due):
                multiply(k)
            multiplied = due
            if issued[0] == len(stream_order):
                for tile_i in range(stored, max(collected - TILES, 0)):
                    store(tile_i)
                stored = max(collected - TILES, stored)

        while multiplied < BLOCKS - TAIL - 2:
            multiply(multiplied)
            multiplied += 1
        for k in range(collected, multiplied):
            collect(k)
        collected = multiplied
        for i in range(TAIL * BLOCK_BANKS):
            k = BLOCKS - TAIL + i // BLOCK_BANKS
            fill_bank(k, i % BLOCK_BANKS, i in TAIL_V)
            if i == 0:
                quantise_weight(BLOCKS - TAIL - 1)
            else:
                quantise_weight(BLOCKS - TAIL + (i - 1) // BLOCK_BANKS, BLOCK_BANKS, (i - 1) % BLOCK_BANKS)
            if i == M28 and M28 < M29:
                multiply(multiplied)
                multiplied += 1
            if i == M29:
                while multiplied < BLOCKS - TAIL:
                    multiply(multiplied)
                    multiplied += 1
                for j in range(collected, multiplied):
                    collect(j)
                for tile_i in range(stored, multiplied - TILES):
                    store(tile_i)
            if i == M30:
                multiply(BLOCKS - 2)
        if M30 > 7:
            multiply(BLOCKS - 2)
        multiply(BLOCKS - 1, range(0, BLOCK_PASSES - 2))
        quantise_weight(BLOCKS - 1, BLOCK_BANKS, BLOCK_BANKS - 1)
        multiply(BLOCKS - 1, range(BLOCK_PASSES - 2, BLOCK_PASSES))
        for k in range(BLOCKS - TAIL, BLOCKS):
            collect(k)
        for tile_i in range(TILES - TAIL, TILES):
            store(tile_i)
